import numpy as np
import ml_dtypes


def mxq(x, axis, fmt="e4m3"):
    dtype, down = {"e4m3": (ml_dtypes.float8_e4m3fn, 7), "e5m2": (ml_dtypes.float8_e5m2, 14)}[fmt]
    v = np.moveaxis(np.asarray(x, np.float32).astype(ml_dtypes.bfloat16).astype(np.float64), axis, -1)
    blocks = v.reshape(v.shape[:-1] + (-1, 32))
    amax = np.abs(blocks).max(-1, keepdims=True)
    byte = np.maximum(np.where(amax > 0, np.frexp(amax)[1] - 1 + 127, 0) - down, 1)
    scale = np.exp2(byte - 127.0)
    codes = (blocks / scale).astype(np.float32).astype(dtype).astype(np.float64)
    return np.moveaxis((codes * scale).reshape(v.shape), -1, axis)


WIDE = False


def mx_kscale(k):
    if not WIDE:
        return np.ones(k)
    levels = np.array([10, -10, 5, -5, 0])
    if k % 512:
        return np.exp2(np.random.permutation(np.resize(levels, k // 32))).repeat(32)
    a = np.empty((k // 512, 16))
    for p in range(k // 512):
        a[p, :8] = np.random.permutation(np.resize(levels, 8))
        for g in range(8):
            far = levels[np.abs(levels - a[p, g]) >= 10]
            a[p, g + 8] = far[np.random.randint(len(far))]
    return np.exp2(a.ravel()).repeat(32)


BF16 = ml_dtypes.bfloat16


def bf(x):
    return np.asarray(x, np.float32).astype(BF16)


def f64(x):
    return np.asarray(x).astype(np.float64)


B, S, D, O = 2, 512, 2048, 1024
T = B * S

EPS = 1.0 / 137.0


def setup_inputs():
    s = mx_kscale(T).reshape(B, S, 1)
    u = mx_kscale(O)
    x0 = bf(np.random.standard_normal((B, S, D)) * 0.5)
    k0 = bf(np.random.standard_normal((D, O)) * 0.5)
    bias = bf(np.random.standard_normal(O) * 0.1)
    alpha = bf(1.0 + 0.1 * np.random.standard_normal(1))
    g = bf(np.random.standard_normal((B, S, O)) * np.exp2(np.random.randint(-6, 1, (B, S, 1))) * 4.0 / s * u)
    xf, kf = f64(x0), f64(k0)
    y = xf @ kf
    x_sq = np.sum(xf * xf, axis=-1, keepdims=True)
    k_sq = np.sum(kf * kf, axis=0, keepdims=True)
    return {"x": bf(xf * s),
            "kernel": bf(kf / u),
            "bias": bias,
            "alpha": alpha,
            "y": np.asarray(y, np.float32),
            "x_sq": np.asarray(x_sq, np.float32),
            "k_sq": np.asarray(k_sq, np.float32),
            "grad_out": g}


def reference(x, kernel, bias, alpha, y, x_sq, k_sq, grad_out):
    xf = f64(x).reshape(T, D)
    kf = f64(kernel)
    yf = f64(y).reshape(T, O)
    den = f64(x_sq).reshape(T, 1) + f64(k_sq).reshape(1, O) - 2.0 * yf + EPS
    r = yf / den
    scale = (np.sqrt(float(O)) / np.log1p(float(O))) ** f64(alpha)[0]
    g = f64(grad_out).reshape(T, O) * scale
    dy = g * (2.0 * r * (1.0 + r))
    gr2 = g * (r * r)
    a = np.sum(gr2, axis=1)
    c = np.sum(gr2, axis=0)
    dx = (mxq(dy, 1, "e5m2") @ mxq(kf, 1, "e4m3").T) - 2.0 * xf * a[:, None]
    dk = (mxq(xf, 0, "e4m3").T @ mxq(dy, 0, "e5m2")) - 2.0 * kf * c[None, :]
    return dx.reshape(B, S, D), dk

@@ -1,0 +1,369 @@
+from contextlib import ExitStack
+
+import concourse.mybir as mybir
+from concourse.masks import make_identity
+
+F32 = mybir.dt.float32
+BF16 = mybir.dt.bfloat16
+U32 = mybir.dt.uint32
+U8 = mybir.dt.uint8
+E4 = mybir.dt.float8_e4m3fn_x4
+E5 = mybir.dt.float8_e5m2_x4
+ALU = mybir.AluOpType
+ACT = mybir.ActivationFunctionType
+
+T, D, O = 1024, 2048, 1024
+P = 128
+FLOPS = 2 * 2 * T * D * O
+EPS = 1.0 / 137.0
+LN_BASE = 1.5295229208621908
+
+MANUAL = True
+V_KC = (3, 7, 11, 15)
+EARLY = {5: [(0, 0), (0, 1)], 6: [(1, 0), (1, 1)], 7: [(2, 0), (2, 1)]}
+PRE = 3
+RES_TAGS = ("res", "a", "q", "il", "il")
+KC_TAGS = ("kc", "y")
+DCP = 2
+BUFS = {"res": 3, "a": 3, "q": 2, "il": 6, "kc": 2, "y": 3}
+
+
+def tile_yatnmn_v_kernel(tc, x, kernel, bias, alpha, y, x_sq, k_sq, grad_out, out_0, out_1):
+    nc = tc.nc
+    with ExitStack() as ctx:
+        keep = ctx.enter_context(tc.tile_pool(name="keep", bufs=1))
+        work = ctx.enter_context(tc.tile_pool(name="work", bufs=2))
+        ps_c = ctx.enter_context(tc.psum_pool(name="ps_c", bufs=1))
+        ps_t = ctx.enter_context(tc.psum_pool(name="ps_t", bufs=2))
+        ps_o = ctx.enter_context(tc.psum_pool(name="ps_o", bufs=4))
+        if MANUAL:
+            ctx.enter_context(tc.manual_schedule())
+
+        ident = keep.tile([P, P], F32, name="ident")
+        ones = keep.tile([P, P], F32, name="ones")
+        xsq_t = keep.tile([P, 2, 4], F32, name="xsq_t")
+        xe = keep.tile([P, 8], F32, name="xe")
+        alpha_b = keep.tile([P, 1], BF16, name="alpha_b")
+        sc1 = keep.tile([P, 1], F32, name="sc1")
+        scale2 = keep.tile([P, 1], F32, name="scale2")
+        neg_a = keep.tile([P, 8], F32, name="neg_a")
+        x_raw = [[keep.tile([P, 4, 1024], BF16, name="x_raw%d%d" % (g, e)) for e in range(2)] for g in range(2)]
+        k_raw = [keep.tile([P, 4, O], BF16, name="k_raw%d" % c) for c in range(4)]
+        dy_raw = [keep.tile([P, 4, O], BF16, name="dy_raw%d" % g) for g in range(2)]
+        kt_q = [keep.tile([P, D], U32, name="kt_q%d" % g, align_bytes=64) for g in range(2)]
+        kt_s = [keep.tile([P, D], U8, name="kt_s%d" % g, align_bytes=64) for g in range(2)]
+        x_q = [keep.tile([P, D], U32, name="x_q%d" % g, align_bytes=64) for g in range(2)]
+        x_s = [keep.tile([P, D], U8, name="x_s%d" % g, align_bytes=64) for g in range(2)]
+        dy_q = [keep.tile([P, O], U32, name="dy_q%d" % g, align_bytes=64) for g in range(2)]
+        dy_s = [keep.tile([P, O], U8, name="dy_s%d" % g, align_bytes=64) for g in range(2)]
+        dyt_q = keep.tile([P, 8, 256], U32, name="dyt_q", align_bytes=64)
+        dyt_s = keep.tile([P, 8, 256], U8, name="dyt_s", align_bytes=64)
+        pc = [ps_c.tile([P, 512], F32, name="pc%d" % h) for h in range(2)]
+        ksqb = [work.tile([P, 512], F32, name="ksqb%d" % h, tag="cb%d" % h, bufs=1) for h in range(2)]
+
+        y_v = [y[g].rearrange("(p j) o -> p j o", j=4) for g in range(2)]
+        g_v = [grad_out[g].rearrange("(p j) o -> p j o", j=4) for g in range(2)]
+        x_v = [x[g].rearrange("(p j) d -> p j d", j=4) for g in range(2)]
+        o0_v = [out_0[g].rearrange("(p j) d -> p j d", j=4) for g in range(2)]
+        k_v = kernel.rearrange("(n p) o -> p n o", p=P)
+        o1_v = out_1.rearrange("(n p) o -> p n o", p=P)
+        ksq_v = k_sq.rearrange("a o -> (a o)")
+
+        y_t = {}
+        g_t = {}
+        a_t = {}
+        q_t = {}
+        st = {"q": [], "res": 0, "kc": 0}
+        HALVES = ((0, 512), (512, 1024))
+
+        def later(job):
+            st["q"] = st["q"] + [job]
+
+        def fill(k):
+            for job in st["q"][:k]:
+                job()
+            st["q"] = st["q"][k:]
+
+        def quant(out, scales, in_):
+            return lambda: nc.vector.quantize_mx(out=out, scales=scales, in_=in_)
+
+        def f4_tile(kind, tags):
+            tag = tags[st[kind] % len(tags)]
+            st[kind] += 1
+            return work.tile([P, 1024], F32, name=kind, tag=tag, bufs=BUFS[tag], align_bytes=64)
+
+        def new_slice(s):
+            y_t[s] = work.tile([P, O], F32, name="y_t", tag="y", bufs=3, align_bytes=64)
+            g_t[s] = work.tile([P, O], BF16, name="g_t", tag="g", bufs=3)
+
+        def load_y(s, lo=0, hi=O):
+            nc.sync.dma_start(out=y_t[s][:, lo:hi], in_=y_v[s // 4][:, s % 4, lo:hi])
+
+        def load_g(s):
+            nc.sync.dma_start(out=g_t[s][:], in_=g_v[s // 4][:, s % 4, :])
+
+        def load_slice(s):
+            new_slice(s)
+            load_y(s)
+            load_g(s)
+
+        def load_k(c):
+            nc.sync.dma_start(out=k_raw[c][:], in_=k_v[:, 4 * c : 4 * c + 4, :])
+
+        def load_x(g, e):
+            nc.sync.dma_start(out=x_raw[g][e][:], in_=x_v[g][:, :, 1024 * e : 1024 * e + 1024])
+
+        def e1(s, h):
+            lo, hi = HALVES[h]
+            nc.vector.scalar_tensor_tensor(
+                out=a_t[s][:, lo:hi], in0=y_t[s][:, lo:hi], scalar=-2.0, in1=ksqb[h][:], op0=ALU.mult, op1=ALU.add
+            )
+
+        def rr(s, lo=0, hi=O):
+            nc.scalar.activation(
+                out=a_t[s][:, lo:hi], in_=a_t[s][:, lo:hi], func=ACT.Abs_reciprocal_sqrt, bias=xe[:, s : s + 1]
+            )
+            nc.scalar.activation(out=a_t[s][:, lo:hi], in_=a_t[s][:, lo:hi], func=ACT.Square)
+
+        def e3(s, lo=0, hi=O):
+            nc.vector.tensor_tensor(out=y_t[s][:, lo:hi], in0=y_t[s][:, lo:hi], in1=a_t[s][:, lo:hi], op=ALU.mult)
+
+        def e4(s, lo=0, hi=O):
+            nc.vector.scalar_tensor_tensor(
+                out=q_t[s][:, lo:hi], in0=g_t[s][:, lo:hi], scalar=scale2[:, 0:1], in1=y_t[s][:, lo:hi],
+                op0=ALU.mult, op1=ALU.mult,
+            )
+
+        def e6(s):
+            nc.vector.scalar_tensor_tensor(
+                out=a_t[s][:], in0=q_t[s][:], scalar=-1.0, in1=y_t[s][:], op0=ALU.mult, op1=ALU.mult,
+                accum_out=neg_a[:, s : s + 1],
+            )
+
+        def e5(s):
+            nc.vector.scalar_tensor_tensor(
+                out=dy_raw[s // 4][:, s % 4, :], in0=y_t[s][:], scalar=1.0, in1=q_t[s][:], op0=ALU.add, op1=ALU.mult
+            )
+
+        def csum(s):
+            for h in range(2):
+                nc.tensor.matmul(
+                    out=pc[h][:], lhsT=ones[:], rhs=a_t[s][:, 512 * h : 512 * h + 512], start=(s == 0), stop=(s == 7)
+                )
+
+        def kernel_group(c, gp):
+            kti = work.tile([P, 512, 4], BF16, name="kti", tag="il", bufs=6, align_bytes=64)
+            ktw = kti[:].rearrange("m d t -> m (d t)").bitcast(F32).rearrange("m (d u) -> m d u", u=2)
+            for b in range(2):
+                pt = ps_t.tile([P, 4, P], F32, name="pt", tag="pt")
+                for n2 in range(2):
+                    words = k_raw[c][:, 2 * b + n2, :].bitcast(F32)
+                    for u in range(2):
+                        nc.tensor.transpose(pt[:, 2 * n2 + u, :], words[:, 256 * gp + u : 256 * gp + 256 : 2], ident[:])
+                nc.scalar.copy(
+                    out=ktw[:, 256 * b : 256 * b + 256, :].rearrange("m (n i) u -> m n i u", n=2),
+                    in_=pt[:].rearrange("m (n u) i -> m n i u", u=2),
+                )
+            cols = slice(512 * c, 512 * c + 512)
+            later(quant(kt_q[gp][:, cols].bitcast(E4), kt_s[gp][:, cols], kti[:].rearrange("m d t -> m (d t)")))
+
+        def x_chunk(g, c):
+            xi = work.tile([P, 512, 4], BF16, name="xi", tag="il", bufs=6, align_bytes=64)
+            cols = slice(512 * c, 512 * c + 512)
+            src = x_raw[g][c // 2][:, :, 512 * (c % 2) : 512 * (c % 2) + 512]
+            nc.scalar.copy(out=xi[:], in_=src.rearrange("p j d -> p d j"))
+            later(quant(x_q[g][:, cols].bitcast(E4), x_s[g][:, cols], xi[:].rearrange("p d j -> p (d j)")))
+
+        def dy_chunk(g, c, pieces):
+            w = O // pieces
+            di = work.tile([P, w, 4], BF16, name="di", tag="il", bufs=6, align_bytes=64)
+            cols = slice(w * c, w * c + w)
+            nc.scalar.copy(out=di[:], in_=dy_raw[g][:, :, cols].rearrange("p j o -> p o j"))
+            later(quant(dy_q[g][:, cols].bitcast(E5), dy_s[g][:, cols], di[:].rearrange("p o j -> p (o j)")))
+
+        def dy_transposed(s):
+            words = dy_raw[s // 4][:, s % 4, :].bitcast(F32)
+            pt = ps_t.tile([P, 4, P], F32, name="pt", tag="pt")
+            for gp in range(2):
+                for u in range(2):
+                    nc.tensor.transpose(pt[:, 2 * gp + u, :], words[:, 256 * gp + u : 256 * gp + 256 : 2], ident[:])
+            dti = work.tile([P, 2, P, 4], BF16, name="dti", tag="dti", bufs=2, align_bytes=64)
+            nc.scalar.copy(
+                out=dti[:].rearrange("m g c t -> m (g c t)").bitcast(F32).rearrange("m (g c u) -> m g c u", g=2, u=2),
+                in_=pt[:].rearrange("m (g u) c -> m g c u", u=2),
+            )
+            later(quant(dyt_q[:, s, :].bitcast(E5), dyt_s[:, s, :], dti[:].rearrange("m g c t -> m (g c t)")))
+
+        def mx0(s, h):
+            banks = []
+            for k in range(2):
+                dn = 2 * h + k
+                po = ps_o.tile([P, 512], F32, name="po", tag="po")
+                for gp in range(2):
+                    nc.tensor.matmul_mx(
+                        out=po[:],
+                        lhsT=dyt_q[:, s, 128 * gp : 128 * gp + 128].bitcast(E5),
+                        lhsT_scale=dyt_s[:, s, 128 * gp : 128 * gp + 128],
+                        rhs=kt_q[gp][:, 512 * dn : 512 * dn + 512].bitcast(E4),
+                        rhs_scale=kt_s[gp][:, 512 * dn : 512 * dn + 512],
+                        start=(gp == 0),
+                        stop=(gp == 1),
+                    )
+                banks = banks + [po]
+            return banks
+
+        def ev0(s, h, banks, split=False):
+            g, j = divmod(s, 4)
+            res = f4_tile("res", RES_TAGS)
+            for k in range(2):
+                nc.vector.scalar_tensor_tensor(
+                    out=res[:, 512 * k : 512 * k + 512],
+                    in0=x_raw[g][h][:, j, 512 * k : 512 * k + 512],
+                    scalar=neg_a[:, s : s + 1],
+                    in1=banks[k][:],
+                    op0=ALU.mult,
+                    op1=ALU.add,
+                )
+                if split:
+                    lo = 1024 * h + 512 * k
+                    nc.sync.dma_start(out=o0_v[g][:, j, lo : lo + 512], in_=res[:, 512 * k : 512 * k + 512])
+            if not split:
+                nc.sync.dma_start(out=o0_v[g][:, j, 1024 * h : 1024 * h + 1024], in_=res[:])
+
+        kc_t = {}
+
+        def kc_make(n):
+            c, i = divmod(n, 4)
+            kc_t[n] = f4_tile("kc", KC_TAGS)
+            if n in V_KC:
+                for h in range(2):
+                    nc.vector.tensor_tensor(
+                        out=kc_t[n][:, 512 * h : 512 * h + 512], in0=k_raw[c][:, i, 512 * h : 512 * h + 512],
+                        in1=pc[h][:], op=ALU.mult,
+                    )
+            else:
+                nc.gpsimd.tensor_tensor(out=kc_t[n][:], in0=k_raw[c][:, i, :], in1=neg_cb[:], op=ALU.mult)
+
+        def mx1(n):
+            banks = []
+            for h in range(2):
+                po = ps_o.tile([P, 512], F32, name="po", tag="po")
+                for g in range(2):
+                    nc.tensor.matmul_mx(
+                        out=po[:],
+                        lhsT=x_q[g][:, 128 * n : 128 * n + 128].bitcast(E4),
+                        lhsT_scale=x_s[g][:, 128 * n : 128 * n + 128],
+                        rhs=dy_q[g][:, 512 * h : 512 * h + 512].bitcast(E5),
+                        rhs_scale=dy_s[g][:, 512 * h : 512 * h + 512],
+                        start=(g == 0),
+                        stop=(g == 1),
+                    )
+                banks = banks + [po]
+            return banks
+
+        def ev1(n, banks, split=False):
+            res = f4_tile("res", RES_TAGS)
+            for h in range(2):
+                cols = slice(512 * h, 512 * h + 512)
+                nc.vector.tensor_tensor(out=res[:, cols], in0=banks[h][:], in1=kc_t[n][:, cols], op=ALU.add)
+                if split:
+                    nc.sync.dma_start(out=o1_v[:, n, cols], in_=res[:, cols])
+            if not split:
+                nc.sync.dma_start(out=o1_v[:, n, :], in_=res[:])
+
+        new_slice(0)
+        new_slice(1)
+        with nc.allow_non_contiguous_dma(reason="small vectors"):
+            nc.sync.dma_start(out=ksqb[0][:], in_=ksq_v[0:512].partition_broadcast(P))
+            load_y(0, 0, 512)
+            nc.sync.dma_start(out=xsq_t[:], in_=x_sq.rearrange("g (p j) a -> p g (j a)", j=4))
+            nc.sync.dma_start(out=ksqb[1][:], in_=ksq_v[512:1024].partition_broadcast(P))
+            load_y(0, 512, 1024)
+            nc.sync.dma_start(out=alpha_b[:], in_=alpha.partition_broadcast(P))
+        load_y(1)
+        load_g(0)
+        load_g(1)
+        load_k(0)
+        load_x(0, 0)
+        load_slice(2)
+        load_k(1)
+        load_x(0, 1)
+
+        make_identity(nc, ident[:])
+        nc.vector.memset(ones[:], 1.0)
+        nc.vector.tensor_scalar_add(xe[:], xsq_t[:].rearrange("p g j -> p (g j)"), EPS)
+        a_t[0] = work.tile([P, O], F32, name="a_t", tag="a", bufs=3, align_bytes=64)
+        for h in range(2):
+            e1(0, h)
+            rr(0, HALVES[h][0], HALVES[h][1])
+            if h == 0:
+                nc.scalar.activation(out=sc1[:], in_=alpha_b[:], func=ACT.Exp, scale=LN_BASE)
+        nc.vector.tensor_scalar_mul(scale2[:], sc1[:], 2.0)
+
+        for s in range(8):
+            early = [(sl, h, mx0(sl, h)) for sl, h in EARLY.get(s, ())]
+            if s + 1 < 8:
+                a_t[s + 1] = work.tile([P, O], F32, name="a_t", tag="a", bufs=3, align_bytes=64)
+                e1(s + 1, 0)
+                e1(s + 1, 1)
+                rr(s + 1)
+            q_t[s] = work.tile([P, O], F32, name="q_t", tag="q", bufs=2, align_bytes=64)
+            if s == 0:
+                e3(0, 0, 512)
+                e3(0, 512, 1024)
+                e4(0, 0, 512)
+                e4(0, 512, 1024)
+            else:
+                e3(s)
+                fill(1)
+                e4(s)
+                fill(1)
+            e6(s)
+            e5(s)
+            fill(9)
+            if s + 3 < 8:
+                load_slice(s + 3)
+            if s == 0:
+                load_k(2)
+                load_k(3)
+            if s == 1:
+                load_x(1, 0)
+                load_x(1, 1)
+            if s < 4:
+                kernel_group(s, 0)
+                kernel_group(s, 1)
+            x_chunk(s // 4, s % 4)
+            if s in (4, 5):
+                dy_chunk(0, s - 4, 2)
+            csum(s)
+            dy_transposed(s)
+            for sl, h, banks in early:
+                ev0(sl, h, banks)
+
+        done0 = [sh for v in EARLY.values() for sh in v]
+        held = [(s, h) for s in range(8) for h in range(2) if (s, h) not in done0]
+        neg_cb = work.tile([P, O], F32, name="neg_cb", tag="ncb", bufs=1)
+        dy_chunk(1, 0, DCP)
+        for h in range(2):
+            nc.scalar.copy(out=neg_cb[:, 512 * h : 512 * h + 512], in_=pc[h][:])
+        kc_make(0)
+        kc_make(1)
+        for c in range(1, DCP):
+            dy_chunk(1, c, DCP)
+        fill(1)
+        for k, (s, h) in enumerate(held[:PRE]):
+            ev0(s, h, mx0(s, h))
+            if k == 0:
+                fill(1)
+        held = held[PRE:]
+        fill(9)
+        total = len(held)
+        done = 0
+        for n in range(16):
+            while (done + 1) * 16 <= n * total + 8:
+                s, h = held[done]
+                ev0(s, h, mx0(s, h))
+                done += 1
+            ev1(n, mx1(n), split=(n == 15))
+            if n + 2 < 16:
+                kc_make(n + 2)

@@ -19,12 +19,16 @@ EPS = 1.0 / 137.0
 LN_BASE = 1.5295229208621908
 
 MANUAL = True
-V_KC = (3, 7, 11, 15)
-EARLY = {5: [(0, 0), (0, 1)], 6: [(1, 0), (1, 1)], 7: [(2, 0), (2, 1)]}
-PRE = 3
+V_KC = (5, 10, 15)
+EARLY = {6: [(0, 0), (1, 0)], 7: [(2, 0), (3, 0)]}
+PRE = 4
 RES_TAGS = ("res", "a", "q", "il", "il")
 KC_TAGS = ("kc", "y")
 DCP = 2
+KGS = {0: 1, 1: 1, 2: 1, 3: 1, 4: 1, 5: 1, 6: 2}
+XCS = {0: 1, 1: 2, 2: 1, 3: 2, 6: 1, 7: 1}
+DCS = {4: 0, 5: 1}
+WARM = 5
 BUFS = {"res": 3, "a": 3, "q": 2, "il": 6, "kc": 2, "y": 3}
 
 
@@ -34,8 +38,7 @@ def tile_yatnmn_v_kernel(tc, x, kernel, bias, alpha, y, x_sq, k_sq, grad_out, ou
         keep = ctx.enter_context(tc.tile_pool(name="keep", bufs=1))
         work = ctx.enter_context(tc.tile_pool(name="work", bufs=2))
         ps_c = ctx.enter_context(tc.psum_pool(name="ps_c", bufs=1))
-        ps_t = ctx.enter_context(tc.psum_pool(name="ps_t", bufs=2))
-        ps_o = ctx.enter_context(tc.psum_pool(name="ps_o", bufs=4))
+        ps_b = ctx.enter_context(tc.psum_pool(name="ps_b", bufs=6))
         if MANUAL:
             ctx.enter_context(tc.manual_schedule())
 
@@ -73,7 +76,7 @@ def tile_yatnmn_v_kernel(tc, x, kernel, bias, alpha, y, x_sq, k_sq, grad_out, ou
         g_t = {}
         a_t = {}
         q_t = {}
-        st = {"q": [], "res": 0, "kc": 0}
+        st = {"q": [], "res": 0, "kc": 0, "kg": 0, "xc": 0}
         HALVES = ((0, 512), (512, 1024))
 
         def later(job):
@@ -113,16 +116,19 @@ def tile_yatnmn_v_kernel(tc, x, kernel, bias, alpha, y, x_sq, k_sq, grad_out, ou
         def load_x(g, e):
             nc.sync.dma_start(out=x_raw[g][e][:], in_=x_v[g][:, :, 1024 * e : 1024 * e + 1024])
 
-        def e1(s, h):
+        def e1(s, h, row=None):
             lo, hi = HALVES[h]
             nc.vector.scalar_tensor_tensor(
-                out=a_t[s][:, lo:hi], in0=y_t[s][:, lo:hi], scalar=-2.0, in1=ksqb[h][:], op0=ALU.mult, op1=ALU.add
+                out=a_t[s][:, lo:hi], in0=y_t[s][:, lo:hi], scalar=-2.0, in1=(ksqb[h][:] if row is None else row[:]),
+                op0=ALU.mult, op1=ALU.add,
             )
 
-        def rr(s, lo=0, hi=O):
+        def rs(s, lo=0, hi=O):
             nc.scalar.activation(
                 out=a_t[s][:, lo:hi], in_=a_t[s][:, lo:hi], func=ACT.Abs_reciprocal_sqrt, bias=xe[:, s : s + 1]
             )
+
+        def sq(s, lo=0, hi=O):
             nc.scalar.activation(out=a_t[s][:, lo:hi], in_=a_t[s][:, lo:hi], func=ACT.Square)
 
         def e3(s, lo=0, hi=O):
@@ -154,18 +160,22 @@ def tile_yatnmn_v_kernel(tc, x, kernel, bias, alpha, y, x_sq, k_sq, grad_out, ou
         def kernel_group(c, gp):
             kti = work.tile([P, 512, 4], BF16, name="kti", tag="il", bufs=6, align_bytes=64)
             ktw = kti[:].rearrange("m d t -> m (d t)").bitcast(F32).rearrange("m (d u) -> m d u", u=2)
+            cols = slice(512 * c, 512 * c + 512)
+            jobs = []
             for b in range(2):
-                pt = ps_t.tile([P, 4, P], F32, name="pt", tag="pt")
+                pt = ps_b.tile([P, 4, P], F32, name="pt", tag="bk")
                 for n2 in range(2):
                     words = k_raw[c][:, 2 * b + n2, :].bitcast(F32)
                     for u in range(2):
                         nc.tensor.transpose(pt[:, 2 * n2 + u, :], words[:, 256 * gp + u : 256 * gp + 256 : 2], ident[:])
-                nc.scalar.copy(
-                    out=ktw[:, 256 * b : 256 * b + 256, :].rearrange("m (n i) u -> m n i u", n=2),
-                    in_=pt[:].rearrange("m (n u) i -> m n i u", u=2),
-                )
-            cols = slice(512 * c, 512 * c + 512)
-            later(quant(kt_q[gp][:, cols].bitcast(E4), kt_s[gp][:, cols], kti[:].rearrange("m d t -> m (d t)")))
+                jobs = jobs + [copy_job(
+                    ktw[:, 256 * b : 256 * b + 256, :].rearrange("m (n i) u -> m n i u", n=2),
+                    pt[:].rearrange("m (n u) i -> m n i u", u=2),
+                )]
+            return jobs, quant(kt_q[gp][:, cols].bitcast(E4), kt_s[gp][:, cols], kti[:].rearrange("m d t -> m (d t)"))
+
+        def copy_job(out, in_):
+            return lambda: nc.scalar.copy(out=out, in_=in_)
 
         def x_chunk(g, c):
             xi = work.tile([P, 512, 4], BF16, name="xi", tag="il", bufs=6, align_bytes=64)
@@ -183,7 +193,7 @@ def tile_yatnmn_v_kernel(tc, x, kernel, bias, alpha, y, x_sq, k_sq, grad_out, ou
 
         def dy_transposed(s):
             words = dy_raw[s // 4][:, s % 4, :].bitcast(F32)
-            pt = ps_t.tile([P, 4, P], F32, name="pt", tag="pt")
+            pt = ps_b.tile([P, 4, P], F32, name="pt", tag="bk")
             for gp in range(2):
                 for u in range(2):
                     nc.tensor.transpose(pt[:, 2 * gp + u, :], words[:, 256 * gp + u : 256 * gp + 256 : 2], ident[:])
@@ -198,7 +208,7 @@ def tile_yatnmn_v_kernel(tc, x, kernel, bias, alpha, y, x_sq, k_sq, grad_out, ou
             banks = []
             for k in range(2):
                 dn = 2 * h + k
-                po = ps_o.tile([P, 512], F32, name="po", tag="po")
+                po = ps_b.tile([P, 512], F32, name="po", tag="bk")
                 for gp in range(2):
                     nc.tensor.matmul_mx(
                         out=po[:],
@@ -247,7 +257,7 @@ def tile_yatnmn_v_kernel(tc, x, kernel, bias, alpha, y, x_sq, k_sq, grad_out, ou
         def mx1(n):
             banks = []
             for h in range(2):
-                po = ps_o.tile([P, 512], F32, name="po", tag="po")
+                po = ps_b.tile([P, 512], F32, name="po", tag="bk")
                 for g in range(2):
                     nc.tensor.matmul_mx(
                         out=po[:],
@@ -273,11 +283,13 @@ def tile_yatnmn_v_kernel(tc, x, kernel, bias, alpha, y, x_sq, k_sq, grad_out, ou
 
         new_slice(0)
         new_slice(1)
+        ksq_pad = work.tile([P, O], F32, name="ksq_pad", tag="res", bufs=BUFS["res"], align_bytes=64)
+        nc.vector.memset(ones[:], 1.0)
+        nc.vector.memset(ksq_pad[:], 0.0)
         with nc.allow_non_contiguous_dma(reason="small vectors"):
-            nc.sync.dma_start(out=ksqb[0][:], in_=ksq_v[0:512].partition_broadcast(P))
+            nc.sync.dma_start(out=ksq_pad[0:1, :], in_=k_sq)
             load_y(0, 0, 512)
             nc.sync.dma_start(out=xsq_t[:], in_=x_sq.rearrange("g (p j) a -> p g (j a)", j=4))
-            nc.sync.dma_start(out=ksqb[1][:], in_=ksq_v[512:1024].partition_broadcast(P))
             load_y(0, 512, 1024)
             nc.sync.dma_start(out=alpha_b[:], in_=alpha.partition_broadcast(P))
         load_y(1)
@@ -290,23 +302,52 @@ def tile_yatnmn_v_kernel(tc, x, kernel, bias, alpha, y, x_sq, k_sq, grad_out, ou
         load_x(0, 1)
 
         make_identity(nc, ident[:])
-        nc.vector.memset(ones[:], 1.0)
+        if WARM:
+            pw = ps_b.tile([P, 512], F32, name="pw", tag="bk")
+            for k in range(WARM):
+                nc.tensor.matmul(out=pw[:, 0:P], lhsT=ones[:], rhs=ones[:], start=True, stop=True)
+        rows = []
+        for h in range(2):
+            pk = ps_b.tile([P, 512], F32, name="pk", tag="bk")
+            nc.tensor.matmul(out=pk[:], lhsT=ones[:], rhs=ksq_pad[:, 512 * h : 512 * h + 512], start=True, stop=True)
+            rows = rows + [pk]
         nc.vector.tensor_scalar_add(xe[:], xsq_t[:].rearrange("p g j -> p (g j)"), EPS)
         a_t[0] = work.tile([P, O], F32, name="a_t", tag="a", bufs=3, align_bytes=64)
+        nc.scalar.activation(out=sc1[:], in_=alpha_b[:], func=ACT.Exp, scale=LN_BASE)
         for h in range(2):
-            e1(0, h)
-            rr(0, HALVES[h][0], HALVES[h][1])
-            if h == 0:
-                nc.scalar.activation(out=sc1[:], in_=alpha_b[:], func=ACT.Exp, scale=LN_BASE)
+            e1(0, h, rows[h])
+            rs(0, HALVES[h][0], HALVES[h][1])
+            sq(0, HALVES[h][0], HALVES[h][1])
         nc.vector.tensor_scalar_mul(scale2[:], sc1[:], 2.0)
 
         for s in range(8):
-            early = [(sl, h, mx0(sl, h)) for sl, h in EARLY.get(s, ())]
+            sjobs = []
+            qjobs = []
+            for k in range(KGS.get(s, 0)):
+                jobs, qj = kernel_group(st["kg"] // 2, st["kg"] % 2)
+                st["kg"] += 1
+                sjobs = sjobs + jobs
+                qjobs = qjobs + [qj]
             if s + 1 < 8:
                 a_t[s + 1] = work.tile([P, O], F32, name="a_t", tag="a", bufs=3, align_bytes=64)
-                e1(s + 1, 0)
-                e1(s + 1, 1)
-                rr(s + 1)
+                e1(s + 1, 0, rows[0] if s == 0 else None)
+                e1(s + 1, 1, rows[1] if s == 0 else None)
+                if s == 0:
+                    rs(1)
+                    for h in range(2):
+                        nc.scalar.copy(out=ksqb[h][:], in_=rows[h][:])
+                    sq(1)
+                else:
+                    for job in sjobs[:1]:
+                        job()
+                    rs(s + 1)
+                    for job in sjobs[1:2]:
+                        job()
+                    sq(s + 1)
+                    sjobs = sjobs[2:]
+            for job in sjobs:
+                job()
+            early = [(sl, h, mx0(sl, h)) for sl, h in EARLY.get(s, ())]
             q_t[s] = work.tile([P, O], F32, name="q_t", tag="q", bufs=2, align_bytes=64)
             if s == 0:
                 e3(0, 0, 512)
@@ -321,6 +362,8 @@ def tile_yatnmn_v_kernel(tc, x, kernel, bias, alpha, y, x_sq, k_sq, grad_out, ou
             e6(s)
             e5(s)
             fill(9)
+            for qj in qjobs:
+                later(qj)
             if s + 3 < 8:
                 load_slice(s + 3)
             if s == 0:
@@ -329,16 +372,15 @@ def tile_yatnmn_v_kernel(tc, x, kernel, bias, alpha, y, x_sq, k_sq, grad_out, ou
             if s == 1:
                 load_x(1, 0)
                 load_x(1, 1)
-            if s < 4:
-                kernel_group(s, 0)
-                kernel_group(s, 1)
-            x_chunk(s // 4, s % 4)
-            if s in (4, 5):
-                dy_chunk(0, s - 4, 2)
-            csum(s)
-            dy_transposed(s)
+            for k in range(XCS.get(s, 0)):
+                x_chunk(st["xc"] // 4, st["xc"] % 4)
+                st["xc"] += 1
+            if s in DCS:
+                dy_chunk(0, DCS[s], 2)
             for sl, h, banks in early:
                 ev0(sl, h, banks)
+            csum(s)
+            dy_transposed(s)
 
         done0 = [sh for v in EARLY.values() for sh in v]
         held = [(s, h) for s in range(8) for h in range(2) if (s, h) not in done0]

@@ -19,15 +19,16 @@ EPS = 1.0 / 137.0
 LN_BASE = 1.5295229208621908
 
 MANUAL = True
-V_KC = (5, 10, 15)
+V_KC = (8, 15)
 EARLY = {6: [(0, 0), (1, 0)], 7: [(2, 0), (3, 0)]}
 PRE = 4
 RES_TAGS = ("res", "a", "q", "il", "il")
 KC_TAGS = ("kc", "y")
-DCP = 2
+DCP = 4
 KGS = {0: 1, 1: 1, 2: 1, 3: 1, 4: 1, 5: 1, 6: 2}
 XCS = {0: 1, 1: 2, 2: 1, 3: 2, 6: 1, 7: 1}
 DCS = {4: 0, 5: 1}
+G_SPLIT = 4
 WARM = 5
 BUFS = {"res": 3, "a": 3, "q": 2, "il": 6, "kc": 2, "y": 3}
 
@@ -181,14 +182,19 @@ def tile_yatnmn_v_kernel(tc, x, kernel, bias, alpha, y, x_sq, k_sq, grad_out, ou
             xi = work.tile([P, 512, 4], BF16, name="xi", tag="il", bufs=6, align_bytes=64)
             cols = slice(512 * c, 512 * c + 512)
             src = x_raw[g][c // 2][:, :, 512 * (c % 2) : 512 * (c % 2) + 512]
-            nc.scalar.copy(out=xi[:], in_=src.rearrange("p j d -> p d j"))
+            nc.scalar.copy(
+                out=xi[:].rearrange("p (c i) j -> p c j i", i=4), in_=src.rearrange("p j (c i) -> p c j i", i=4)
+            )
             later(quant(x_q[g][:, cols].bitcast(E4), x_s[g][:, cols], xi[:].rearrange("p d j -> p (d j)")))
 
         def dy_chunk(g, c, pieces):
             w = O // pieces
             di = work.tile([P, w, 4], BF16, name="di", tag="il", bufs=6, align_bytes=64)
             cols = slice(w * c, w * c + w)
-            nc.scalar.copy(out=di[:], in_=dy_raw[g][:, :, cols].rearrange("p j o -> p o j"))
+            nc.scalar.copy(
+                out=di[:].rearrange("p (c i) j -> p c j i", i=4),
+                in_=dy_raw[g][:, :, cols].rearrange("p j (c i) -> p c j i", i=4),
+            )
             later(quant(dy_q[g][:, cols].bitcast(E5), dy_s[g][:, cols], di[:].rearrange("p o j -> p (o j)")))
 
         def dy_transposed(s):
@@ -251,6 +257,10 @@ def tile_yatnmn_v_kernel(tc, x, kernel, bias, alpha, y, x_sq, k_sq, grad_out, ou
                         out=kc_t[n][:, 512 * h : 512 * h + 512], in0=k_raw[c][:, i, 512 * h : 512 * h + 512],
                         in1=pc[h][:], op=ALU.mult,
                     )
+            elif n < G_SPLIT:
+                for h in range(2):
+                    cols = slice(512 * h, 512 * h + 512)
+                    nc.gpsimd.tensor_tensor(out=kc_t[n][:, cols], in0=k_raw[c][:, i, cols], in1=neg_cb[:, cols], op=ALU.mult)
             else:
                 nc.gpsimd.tensor_tensor(out=kc_t[n][:], in0=k_raw[c][:, i, :], in1=neg_cb[:], op=ALU.mult)
 
@@ -283,15 +293,18 @@ def tile_yatnmn_v_kernel(tc, x, kernel, bias, alpha, y, x_sq, k_sq, grad_out, ou
 
         new_slice(0)
         new_slice(1)
-        ksq_pad = work.tile([P, O], F32, name="ksq_pad", tag="res", bufs=BUFS["res"], align_bytes=64)
+        ksq_pad = [work.tile([P, 512], F32, name="ksq_pad%d" % h, tag="res", bufs=BUFS["res"], align_bytes=64)
+                   for h in range(2)]
+        nc.vector.memset(ksq_pad[0][:], 0.0)
+        nc.gpsimd.memset(ksq_pad[1][:], 0.0)
         nc.vector.memset(ones[:], 1.0)
-        nc.vector.memset(ksq_pad[:], 0.0)
         with nc.allow_non_contiguous_dma(reason="small vectors"):
-            nc.sync.dma_start(out=ksq_pad[0:1, :], in_=k_sq)
-            load_y(0, 0, 512)
-            nc.sync.dma_start(out=xsq_t[:], in_=x_sq.rearrange("g (p j) a -> p g (j a)", j=4))
-            load_y(0, 512, 1024)
             nc.sync.dma_start(out=alpha_b[:], in_=alpha.partition_broadcast(P))
+            nc.sync.dma_start(out=xsq_t[:], in_=x_sq.rearrange("g (p j) a -> p g (j a)", j=4))
+            load_y(0, 0, 512)
+            nc.sync.dma_start(out=ksq_pad[0][0:1, :], in_=k_sq[:, 0:512])
+            nc.sync.dma_start(out=ksq_pad[1][0:1, :], in_=k_sq[:, 512:1024])
+            load_y(0, 512, 1024)
         load_y(1)
         load_g(0)
         load_g(1)
@@ -309,7 +322,7 @@ def tile_yatnmn_v_kernel(tc, x, kernel, bias, alpha, y, x_sq, k_sq, grad_out, ou
         rows = []
         for h in range(2):
             pk = ps_b.tile([P, 512], F32, name="pk", tag="bk")
-            nc.tensor.matmul(out=pk[:], lhsT=ones[:], rhs=ksq_pad[:, 512 * h : 512 * h + 512], start=True, stop=True)
+            nc.tensor.matmul(out=pk[:], lhsT=ones[:], rhs=ksq_pad[h][:], start=True, stop=True)
             rows = rows + [pk]
         nc.vector.tensor_scalar_add(xe[:], xsq_t[:].rearrange("p g j -> p (g j)"), EPS)
         a_t[0] = work.tile([P, O], F32, name="a_t", tag="a", bufs=3, align_bytes=64)
@@ -380,7 +393,8 @@ def tile_yatnmn_v_kernel(tc, x, kernel, bias, alpha, y, x_sq, k_sq, grad_out, ou
             for sl, h, banks in early:
                 ev0(sl, h, banks)
             csum(s)
-            dy_transposed(s)
+            if s < 7:
+                dy_transposed(s)
 
         done0 = [sh for v in EARLY.values() for sh in v]
         held = [(s, h) for s in range(8) for h in range(2) if (s, h) not in done0]
@@ -390,19 +404,19 @@ def tile_yatnmn_v_kernel(tc, x, kernel, bias, alpha, y, x_sq, k_sq, grad_out, ou
             nc.scalar.copy(out=neg_cb[:, 512 * h : 512 * h + 512], in_=pc[h][:])
         kc_make(0)
         kc_make(1)
+        dy_transposed(7)
         for c in range(1, DCP):
             dy_chunk(1, c, DCP)
         fill(1)
-        for k, (s, h) in enumerate(held[:PRE]):
+        for s, h in held[:PRE]:
             ev0(s, h, mx0(s, h))
-            if k == 0:
-                fill(1)
+            fill(1)
         held = held[PRE:]
         fill(9)
         total = len(held)
         done = 0
         for n in range(16):
-            while (done + 1) * 16 <= n * total + 8:
+            while (done + 1) * 16 <= (n + 1) * total:
                 s, h = held[done]
                 ev0(s, h, mx0(s, h))
                 done += 1

@@ -19,8 +19,8 @@ EPS = 1.0 / 137.0
 LN_BASE = 1.5295229208621908
 
 MANUAL = True
-V_KC = (8, 15)
-EARLY = {6: [(0, 0), (1, 0)], 7: [(2, 0), (3, 0)]}
+V_KC = (5, 10, 15)
+EARLY = {5: [(0, 0), (1, 0)], 6: [(2, 0), (3, 0)], 7: [(4, 0), (5, 0)]}
 PRE = 4
 RES_TAGS = ("res", "a", "q", "il", "il")
 KC_TAGS = ("kc", "y")
@@ -29,6 +29,7 @@ KGS = {0: 1, 1: 1, 2: 1, 3: 1, 4: 1, 5: 1, 6: 2}
 XCS = {0: 1, 1: 2, 2: 1, 3: 2, 6: 1, 7: 1}
 DCS = {4: 0, 5: 1}
 G_SPLIT = 4
+G_E5 = (5, 6)
 WARM = 5
 BUFS = {"res": 3, "a": 3, "q": 2, "il": 6, "kc": 2, "y": 3}
 
@@ -373,7 +374,15 @@ def tile_yatnmn_v_kernel(tc, x, kernel, bias, alpha, y, x_sq, k_sq, grad_out, ou
                 e4(s)
                 fill(1)
             e6(s)
-            e5(s)
+            if s in G_E5:
+                nc.gpsimd.tensor_tensor(
+                    out=dy_raw[s // 4][:, s % 4, :], in0=q_t[s][:], in1=a_t[s][:], op=ALU.subtract
+                )
+                for sl, h, banks in early:
+                    ev0(sl, h, banks)
+                early = []
+            else:
+                e5(s)
             fill(9)
             for qj in qjobs:
                 later(qj)

@@ -19,17 +19,17 @@ EPS = 1.0 / 137.0
 LN_BASE = 1.5295229208621908
 
 MANUAL = True
-V_KC = (5, 10, 15)
-EARLY = {5: [(0, 0), (1, 0)], 6: [(2, 0), (3, 0)], 7: [(4, 0), (5, 0)]}
-PRE = 4
+V_KC = (3, 8, 13)
+EARLY = {4: [(0, 0), (1, 0)], 5: [(2, 0), (3, 0)], 6: [(0, 1), (1, 1)], 7: [(2, 1), (3, 1)]}
+PRE = 3
 RES_TAGS = ("res", "a", "q", "il", "il")
 KC_TAGS = ("kc", "y")
 DCP = 4
-KGS = {0: 1, 1: 1, 2: 1, 3: 1, 4: 1, 5: 1, 6: 2}
-XCS = {0: 1, 1: 2, 2: 1, 3: 2, 6: 1, 7: 1}
-DCS = {4: 0, 5: 1}
+KGS = {0: 1, 1: 2, 2: 2, 3: 2, 4: 1}
+XCS = {0: 1, 1: 1, 2: 1, 3: 1, 4: 1, 5: 1, 6: 1, 7: 1}
+DCS = {4: 0, 6: 1}
 G_SPLIT = 4
-G_E5 = (5, 6)
+G_E5 = (4, 5, 6)
 WARM = 5
 BUFS = {"res": 3, "a": 3, "q": 2, "il": 6, "kc": 2, "y": 3}
 

from contextlib import ExitStack

import concourse.mybir as mybir
from concourse.masks import make_identity

F32 = mybir.dt.float32
BF16 = mybir.dt.bfloat16
U32 = mybir.dt.uint32
U8 = mybir.dt.uint8
E4 = mybir.dt.float8_e4m3fn_x4
E5 = mybir.dt.float8_e5m2_x4
ALU = mybir.AluOpType
ACT = mybir.ActivationFunctionType

T, D, O = 1024, 2048, 1024
P = 128
FLOPS = 2 * 2 * T * D * O
EPS = 1.0 / 137.0
LN_BASE = 1.5295229208621908

MANUAL = True
V_KC = (3, 8, 13)
EARLY = {4: [(0, 0), (1, 0)], 5: [(2, 0), (3, 0)], 6: [(0, 1), (1, 1)], 7: [(2, 1), (3, 1)]}
PRE = 3
RES_TAGS = ("res", "a", "q", "il", "il")
KC_TAGS = ("kc", "y")
DCP = 4
KGS = {0: 1, 1: 2, 2: 2, 3: 2, 4: 1}
XCS = {0: 1, 1: 1, 2: 1, 3: 1, 4: 1, 5: 1, 6: 1, 7: 1}
DCS = {4: 0, 6: 1}
G_SPLIT = 4
G_E5 = (4, 5, 6)
WARM = 5
BUFS = {"res": 3, "a": 3, "q": 2, "il": 6, "kc": 2, "y": 3}


def tile_yatnmn_v_kernel(tc, x, kernel, bias, alpha, y, x_sq, k_sq, grad_out, out_0, out_1):
    nc = tc.nc
    with ExitStack() as ctx:
        keep = ctx.enter_context(tc.tile_pool(name="keep", bufs=1))
        work = ctx.enter_context(tc.tile_pool(name="work", bufs=2))
        ps_c = ctx.enter_context(tc.psum_pool(name="ps_c", bufs=1))
        ps_b = ctx.enter_context(tc.psum_pool(name="ps_b", bufs=6))
        if MANUAL:
            ctx.enter_context(tc.manual_schedule())

        ident = keep.tile([P, P], F32, name="ident")
        ones = keep.tile([P, P], F32, name="ones")
        xsq_t = keep.tile([P, 2, 4], F32, name="xsq_t")
        xe = keep.tile([P, 8], F32, name="xe")
        alpha_b = keep.tile([P, 1], BF16, name="alpha_b")
        sc1 = keep.tile([P, 1], F32, name="sc1")
        scale2 = keep.tile([P, 1], F32, name="scale2")
        neg_a = keep.tile([P, 8], F32, name="neg_a")
        x_raw = [[keep.tile([P, 4, 1024], BF16, name="x_raw%d%d" % (g, e)) for e in range(2)] for g in range(2)]
        k_raw = [keep.tile([P, 4, O], BF16, name="k_raw%d" % c) for c in range(4)]
        dy_raw = [keep.tile([P, 4, O], BF16, name="dy_raw%d" % g) for g in range(2)]
        kt_q = [keep.tile([P, D], U32, name="kt_q%d" % g, align_bytes=64) for g in range(2)]
        kt_s = [keep.tile([P, D], U8, name="kt_s%d" % g, align_bytes=64) for g in range(2)]
        x_q = [keep.tile([P, D], U32, name="x_q%d" % g, align_bytes=64) for g in range(2)]
        x_s = [keep.tile([P, D], U8, name="x_s%d" % g, align_bytes=64) for g in range(2)]
        dy_q = [keep.tile([P, O], U32, name="dy_q%d" % g, align_bytes=64) for g in range(2)]
        dy_s = [keep.tile([P, O], U8, name="dy_s%d" % g, align_bytes=64) for g in range(2)]
        dyt_q = keep.tile([P, 8, 256], U32, name="dyt_q", align_bytes=64)
        dyt_s = keep.tile([P, 8, 256], U8, name="dyt_s", align_bytes=64)
        pc = [ps_c.tile([P, 512], F32, name="pc%d" % h) for h in range(2)]
        ksqb = [work.tile([P, 512], F32, name="ksqb%d" % h, tag="cb%d" % h, bufs=1) for h in range(2)]

        y_v = [y[g].rearrange("(p j) o -> p j o", j=4) for g in range(2)]
        g_v = [grad_out[g].rearrange("(p j) o -> p j o", j=4) for g in range(2)]
        x_v = [x[g].rearrange("(p j) d -> p j d", j=4) for g in range(2)]
        o0_v = [out_0[g].rearrange("(p j) d -> p j d", j=4) for g in range(2)]
        k_v = kernel.rearrange("(n p) o -> p n o", p=P)
        o1_v = out_1.rearrange("(n p) o -> p n o", p=P)
        ksq_v = k_sq.rearrange("a o -> (a o)")

        y_t = {}
        g_t = {}
        a_t = {}
        q_t = {}
        st = {"q": [], "res": 0, "kc": 0, "kg": 0, "xc": 0}
        HALVES = ((0, 512), (512, 1024))

        def later(job):
            st["q"] = st["q"] + [job]

        def fill(k):
            for job in st["q"][:k]:
                job()
            st["q"] = st["q"][k:]

        def quant(out, scales, in_):
            return lambda: nc.vector.quantize_mx(out=out, scales=scales, in_=in_)

        def f4_tile(kind, tags):
            tag = tags[st[kind] % len(tags)]
            st[kind] += 1
            return work.tile([P, 1024], F32, name=kind, tag=tag, bufs=BUFS[tag], align_bytes=64)

        def new_slice(s):
            y_t[s] = work.tile([P, O], F32, name="y_t", tag="y", bufs=3, align_bytes=64)
            g_t[s] = work.tile([P, O], BF16, name="g_t", tag="g", bufs=3)

        def load_y(s, lo=0, hi=O):
            nc.sync.dma_start(out=y_t[s][:, lo:hi], in_=y_v[s // 4][:, s % 4, lo:hi])

        def load_g(s):
            nc.sync.dma_start(out=g_t[s][:], in_=g_v[s // 4][:, s % 4, :])

        def load_slice(s):
            new_slice(s)
            load_y(s)
            load_g(s)

        def load_k(c):
            nc.sync.dma_start(out=k_raw[c][:], in_=k_v[:, 4 * c : 4 * c + 4, :])

        def load_x(g, e):
            nc.sync.dma_start(out=x_raw[g][e][:], in_=x_v[g][:, :, 1024 * e : 1024 * e + 1024])

        def e1(s, h, row=None):
            lo, hi = HALVES[h]
            nc.vector.scalar_tensor_tensor(
                out=a_t[s][:, lo:hi], in0=y_t[s][:, lo:hi], scalar=-2.0, in1=(ksqb[h][:] if row is None else row[:]),
                op0=ALU.mult, op1=ALU.add,
            )

        def rs(s, lo=0, hi=O):
            nc.scalar.activation(
                out=a_t[s][:, lo:hi], in_=a_t[s][:, lo:hi], func=ACT.Abs_reciprocal_sqrt, bias=xe[:, s : s + 1]
            )

        def sq(s, lo=0, hi=O):
            nc.scalar.activation(out=a_t[s][:, lo:hi], in_=a_t[s][:, lo:hi], func=ACT.Square)

        def e3(s, lo=0, hi=O):
            nc.vector.tensor_tensor(out=y_t[s][:, lo:hi], in0=y_t[s][:, lo:hi], in1=a_t[s][:, lo:hi], op=ALU.mult)

        def e4(s, lo=0, hi=O):
            nc.vector.scalar_tensor_tensor(
                out=q_t[s][:, lo:hi], in0=g_t[s][:, lo:hi], scalar=scale2[:, 0:1], in1=y_t[s][:, lo:hi],
                op0=ALU.mult, op1=ALU.mult,
            )

        def e6(s):
            nc.vector.scalar_tensor_tensor(
                out=a_t[s][:], in0=q_t[s][:], scalar=-1.0, in1=y_t[s][:], op0=ALU.mult, op1=ALU.mult,
                accum_out=neg_a[:, s : s + 1],
            )

        def e5(s):
            nc.vector.scalar_tensor_tensor(
                out=dy_raw[s // 4][:, s % 4, :], in0=y_t[s][:], scalar=1.0, in1=q_t[s][:], op0=ALU.add, op1=ALU.mult
            )

        def csum(s):
            for h in range(2):
                nc.tensor.matmul(
                    out=pc[h][:], lhsT=ones[:], rhs=a_t[s][:, 512 * h : 512 * h + 512], start=(s == 0), stop=(s == 7)
                )

        def kernel_group(c, gp):
            kti = work.tile([P, 512, 4], BF16, name="kti", tag="il", bufs=6, align_bytes=64)
            ktw = kti[:].rearrange("m d t -> m (d t)").bitcast(F32).rearrange("m (d u) -> m d u", u=2)
            cols = slice(512 * c, 512 * c + 512)
            jobs = []
            for b in range(2):
                pt = ps_b.tile([P, 4, P], F32, name="pt", tag="bk")
                for n2 in range(2):
                    words = k_raw[c][:, 2 * b + n2, :].bitcast(F32)
                    for u in range(2):
                        nc.tensor.transpose(pt[:, 2 * n2 + u, :], words[:, 256 * gp + u : 256 * gp + 256 : 2], ident[:])
                jobs = jobs + [copy_job(
                    ktw[:, 256 * b : 256 * b + 256, :].rearrange("m (n i) u -> m n i u", n=2),
                    pt[:].rearrange("m (n u) i -> m n i u", u=2),
                )]
            return jobs, quant(kt_q[gp][:, cols].bitcast(E4), kt_s[gp][:, cols], kti[:].rearrange("m d t -> m (d t)"))

        def copy_job(out, in_):
            return lambda: nc.scalar.copy(out=out, in_=in_)

        def x_chunk(g, c):
            xi = work.tile([P, 512, 4], BF16, name="xi", tag="il", bufs=6, align_bytes=64)
            cols = slice(512 * c, 512 * c + 512)
            src = x_raw[g][c // 2][:, :, 512 * (c % 2) : 512 * (c % 2) + 512]
            nc.scalar.copy(
                out=xi[:].rearrange("p (c i) j -> p c j i", i=4), in_=src.rearrange("p j (c i) -> p c j i", i=4)
            )
            later(quant(x_q[g][:, cols].bitcast(E4), x_s[g][:, cols], xi[:].rearrange("p d j -> p (d j)")))

        def dy_chunk(g, c, pieces):
            w = O // pieces
            di = work.tile([P, w, 4], BF16, name="di", tag="il", bufs=6, align_bytes=64)
            cols = slice(w * c, w * c + w)
            nc.scalar.copy(
                out=di[:].rearrange("p (c i) j -> p c j i", i=4),
                in_=dy_raw[g][:, :, cols].rearrange("p j (c i) -> p c j i", i=4),
            )
            later(quant(dy_q[g][:, cols].bitcast(E5), dy_s[g][:, cols], di[:].rearrange("p o j -> p (o j)")))

        def dy_transposed(s):
            words = dy_raw[s // 4][:, s % 4, :].bitcast(F32)
            pt = ps_b.tile([P, 4, P], F32, name="pt", tag="bk")
            for gp in range(2):
                for u in range(2):
                    nc.tensor.transpose(pt[:, 2 * gp + u, :], words[:, 256 * gp + u : 256 * gp + 256 : 2], ident[:])
            dti = work.tile([P, 2, P, 4], BF16, name="dti", tag="dti", bufs=2, align_bytes=64)
            nc.scalar.copy(
                out=dti[:].rearrange("m g c t -> m (g c t)").bitcast(F32).rearrange("m (g c u) -> m g c u", g=2, u=2),
                in_=pt[:].rearrange("m (g u) c -> m g c u", u=2),
            )
            later(quant(dyt_q[:, s, :].bitcast(E5), dyt_s[:, s, :], dti[:].rearrange("m g c t -> m (g c t)")))

        def mx0(s, h):
            banks = []
            for k in range(2):
                dn = 2 * h + k
                po = ps_b.tile([P, 512], F32, name="po", tag="bk")
                for gp in range(2):
                    nc.tensor.matmul_mx(
                        out=po[:],
                        lhsT=dyt_q[:, s, 128 * gp : 128 * gp + 128].bitcast(E5),
                        lhsT_scale=dyt_s[:, s, 128 * gp : 128 * gp + 128],
                        rhs=kt_q[gp][:, 512 * dn : 512 * dn + 512].bitcast(E4),
                        rhs_scale=kt_s[gp][:, 512 * dn : 512 * dn + 512],
                        start=(gp == 0),
                        stop=(gp == 1),
                    )
                banks = banks + [po]
            return banks

        def ev0(s, h, banks, split=False):
            g, j = divmod(s, 4)
            res = f4_tile("res", RES_TAGS)
            for k in range(2):
                nc.vector.scalar_tensor_tensor(
                    out=res[:, 512 * k : 512 * k + 512],
                    in0=x_raw[g][h][:, j, 512 * k : 512 * k + 512],
                    scalar=neg_a[:, s : s + 1],
                    in1=banks[k][:],
                    op0=ALU.mult,
                    op1=ALU.add,
                )
                if split:
                    lo = 1024 * h + 512 * k
                    nc.sync.dma_start(out=o0_v[g][:, j, lo : lo + 512], in_=res[:, 512 * k : 512 * k + 512])
            if not split:
                nc.sync.dma_start(out=o0_v[g][:, j, 1024 * h : 1024 * h + 1024], in_=res[:])

        kc_t = {}

        def kc_make(n):
            c, i = divmod(n, 4)
            kc_t[n] = f4_tile("kc", KC_TAGS)
            if n in V_KC:
                for h in range(2):
                    nc.vector.tensor_tensor(
                        out=kc_t[n][:, 512 * h : 512 * h + 512], in0=k_raw[c][:, i, 512 * h : 512 * h + 512],
                        in1=pc[h][:], op=ALU.mult,
                    )
            elif n < G_SPLIT:
                for h in range(2):
                    cols = slice(512 * h, 512 * h + 512)
                    nc.gpsimd.tensor_tensor(out=kc_t[n][:, cols], in0=k_raw[c][:, i, cols], in1=neg_cb[:, cols], op=ALU.mult)
            else:
                nc.gpsimd.tensor_tensor(out=kc_t[n][:], in0=k_raw[c][:, i, :], in1=neg_cb[:], op=ALU.mult)

        def mx1(n):
            banks = []
            for h in range(2):
                po = ps_b.tile([P, 512], F32, name="po", tag="bk")
                for g in range(2):
                    nc.tensor.matmul_mx(
                        out=po[:],
                        lhsT=x_q[g][:, 128 * n : 128 * n + 128].bitcast(E4),
                        lhsT_scale=x_s[g][:, 128 * n : 128 * n + 128],
                        rhs=dy_q[g][:, 512 * h : 512 * h + 512].bitcast(E5),
                        rhs_scale=dy_s[g][:, 512 * h : 512 * h + 512],
                        start=(g == 0),
                        stop=(g == 1),
                    )
                banks = banks + [po]
            return banks

        def ev1(n, banks, split=False):
            res = f4_tile("res", RES_TAGS)
            for h in range(2):
                cols = slice(512 * h, 512 * h + 512)
                nc.vector.tensor_tensor(out=res[:, cols], in0=banks[h][:], in1=kc_t[n][:, cols], op=ALU.add)
                if split:
                    nc.sync.dma_start(out=o1_v[:, n, cols], in_=res[:, cols])
            if not split:
                nc.sync.dma_start(out=o1_v[:, n, :], in_=res[:])

        new_slice(0)
        new_slice(1)
        ksq_pad = [work.tile([P, 512], F32, name="ksq_pad%d" % h, tag="res", bufs=BUFS["res"], align_bytes=64)
                   for h in range(2)]
        nc.vector.memset(ksq_pad[0][:], 0.0)
        nc.gpsimd.memset(ksq_pad[1][:], 0.0)
        nc.vector.memset(ones[:], 1.0)
        with nc.allow_non_contiguous_dma(reason="small vectors"):
            nc.sync.dma_start(out=alpha_b[:], in_=alpha.partition_broadcast(P))
            nc.sync.dma_start(out=xsq_t[:], in_=x_sq.rearrange("g (p j) a -> p g (j a)", j=4))
            load_y(0, 0, 512)
            nc.sync.dma_start(out=ksq_pad[0][0:1, :], in_=k_sq[:, 0:512])
            nc.sync.dma_start(out=ksq_pad[1][0:1, :], in_=k_sq[:, 512:1024])
            load_y(0, 512, 1024)
        load_y(1)
        load_g(0)
        load_g(1)
        load_k(0)
        load_x(0, 0)
        load_slice(2)
        load_k(1)
        load_x(0, 1)

        make_identity(nc, ident[:])
        if WARM:
            pw = ps_b.tile([P, 512], F32, name="pw", tag="bk")
            for k in range(WARM):
                nc.tensor.matmul(out=pw[:, 0:P], lhsT=ones[:], rhs=ones[:], start=True, stop=True)
        rows = []
        for h in range(2):
            pk = ps_b.tile([P, 512], F32, name="pk", tag="bk")
            nc.tensor.matmul(out=pk[:], lhsT=ones[:], rhs=ksq_pad[h][:], start=True, stop=True)
            rows = rows + [pk]
        nc.vector.tensor_scalar_add(xe[:], xsq_t[:].rearrange("p g j -> p (g j)"), EPS)
        a_t[0] = work.tile([P, O], F32, name="a_t", tag="a", bufs=3, align_bytes=64)
        nc.scalar.activation(out=sc1[:], in_=alpha_b[:], func=ACT.Exp, scale=LN_BASE)
        for h in range(2):
            e1(0, h, rows[h])
            rs(0, HALVES[h][0], HALVES[h][1])
            sq(0, HALVES[h][0], HALVES[h][1])
        nc.vector.tensor_scalar_mul(scale2[:], sc1[:], 2.0)

        for s in range(8):
            sjobs = []
            qjobs = []
            for k in range(KGS.get(s, 0)):
                jobs, qj = kernel_group(st["kg"] // 2, st["kg"] % 2)
                st["kg"] += 1
                sjobs = sjobs + jobs
                qjobs = qjobs + [qj]
            if s + 1 < 8:
                a_t[s + 1] = work.tile([P, O], F32, name="a_t", tag="a", bufs=3, align_bytes=64)
                e1(s + 1, 0, rows[0] if s == 0 else None)
                e1(s + 1, 1, rows[1] if s == 0 else None)
                if s == 0:
                    rs(1)
                    for h in range(2):
                        nc.scalar.copy(out=ksqb[h][:], in_=rows[h][:])
                    sq(1)
                else:
                    for job in sjobs[:1]:
                        job()
                    rs(s + 1)
                    for job in sjobs[1:2]:
                        job()
                    sq(s + 1)
                    sjobs = sjobs[2:]
            for job in sjobs:
                job()
            early = [(sl, h, mx0(sl, h)) for sl, h in EARLY.get(s, ())]
            q_t[s] = work.tile([P, O], F32, name="q_t", tag="q", bufs=2, align_bytes=64)
            if s == 0:
                e3(0, 0, 512)
                e3(0, 512, 1024)
                e4(0, 0, 512)
                e4(0, 512, 1024)
            else:
                e3(s)
                fill(1)
                e4(s)
                fill(1)
            e6(s)
            if s in G_E5:
                nc.gpsimd.tensor_tensor(
                    out=dy_raw[s // 4][:, s % 4, :], in0=q_t[s][:], in1=a_t[s][:], op=ALU.subtract
                )
                for sl, h, banks in early:
                    ev0(sl, h, banks)
                early = []
            else:
                e5(s)
            fill(9)
            for qj in qjobs:
                later(qj)
            if s + 3 < 8:
                load_slice(s + 3)
            if s == 0:
                load_k(2)
                load_k(3)
            if s == 1:
                load_x(1, 0)
                load_x(1, 1)
            for k in range(XCS.get(s, 0)):
                x_chunk(st["xc"] // 4, st["xc"] % 4)
                st["xc"] += 1
            if s in DCS:
                dy_chunk(0, DCS[s], 2)
            for sl, h, banks in early:
                ev0(sl, h, banks)
            csum(s)
            if s < 7:
                dy_transposed(s)

        done0 = [sh for v in EARLY.values() for sh in v]
        held = [(s, h) for s in range(8) for h in range(2) if (s, h) not in done0]
        neg_cb = work.tile([P, O], F32, name="neg_cb", tag="ncb", bufs=1)
        dy_chunk(1, 0, DCP)
        for h in range(2):
            nc.scalar.copy(out=neg_cb[:, 512 * h : 512 * h + 512], in_=pc[h][:])
        kc_make(0)
        kc_make(1)
        dy_transposed(7)
        for c in range(1, DCP):
            dy_chunk(1, c, DCP)
        fill(1)
        for s, h in held[:PRE]:
            ev0(s, h, mx0(s, h))
            fill(1)
        held = held[PRE:]
        fill(9)
        total = len(held)
        done = 0
        for n in range(16):
            while (done + 1) * 16 <= (n + 1) * total:
                s, h = held[done]
                ev0(s, h, mx0(s, h))
                done += 1
            ev1(n, mx1(n), split=(n == 15))
            if n + 2 < 16:
                kc_make(n + 2)
